import numpy as np
import ml_dtypes


def mxq(x, axis, fmt="e4m3"):
    dtype, down = {"e4m3": (ml_dtypes.float8_e4m3fn, 7), "e5m2": (ml_dtypes.float8_e5m2, 14)}[fmt]
    v = np.moveaxis(np.asarray(x, np.float32).astype(ml_dtypes.bfloat16).astype(np.float64), axis, -1)
    blocks = v.reshape(v.shape[:-1] + (-1, 32))
    amax = np.abs(blocks).max(-1, keepdims=True)
    byte = np.maximum(np.where(amax > 0, np.frexp(amax)[1] - 1 + 127, 0) - down, 1)
    scale = np.exp2(byte - 127.0)
    codes = (blocks / scale).astype(np.float32).astype(dtype).astype(np.float64)
    return np.moveaxis((codes * scale).reshape(v.shape), -1, axis)


WIDE = False


def mx_kscale(k):
    if not WIDE:
        return np.ones(k)
    levels = np.array([10, -10, 5, -5, 0])
    a = np.random.permutation(np.resize(levels, k // 512 * 4)).reshape(k // 512, 4)
    idx = np.arange(k)
    return np.exp2(a[idx // 512, idx % 128 // 32])


BF16 = ml_dtypes.bfloat16


def bf(x):
    return np.asarray(x, np.float32).astype(BF16)


def f64(x):
    return np.asarray(x).astype(np.float64)


T, D, E, BLK = 8192, 1024, 128, 512
EPS = 1e-05


def setup_inputs():
    s = mx_kscale(D)
    rs = 10.0 ** np.random.uniform(-2.5, 0.5, (T, 1))
    return {"h": bf((np.random.standard_normal((T, D)) + 0.3) * rs),
            "ln_w": bf(np.random.standard_normal(D) * s),
            "ln_b": bf(np.random.standard_normal(D) * 0.3 * s),
            "w_q": bf(np.random.standard_normal((E, D)) * 1.6 / np.sqrt(D) / s),
            "w_k": bf(np.random.standard_normal((E, D)) * 1.6 / np.sqrt(D) / s),
            "w_v": bf(np.random.standard_normal((E, D)) * 1.0 / np.sqrt(D) / s)}


def reference(h, ln_w, ln_b, w_q, w_k, w_v):
    h = f64(h)
    mu = h.mean(-1, keepdims=True)
    var = np.square(h - mu).mean(-1, keepdims=True)
    h_norm = (h - mu) / np.sqrt(var + EPS) * f64(ln_w) + f64(ln_b)
    hq = mxq(h_norm, 1, "e4m3")
    q = hq @ mxq(f64(w_q), 1, "e4m3").T
    k = hq @ mxq(f64(w_k), 1, "e4m3").T
    v = hq @ mxq(f64(w_v), 1, "e4m3").T
    return q, k, v

@@ -1,0 +1,180 @@
+from contextlib import ExitStack
+
+import concourse.mybir as mybir
+from concourse.masks import make_identity
+
+F32 = mybir.dt.float32
+BF16 = mybir.dt.bfloat16
+U32 = mybir.dt.uint32
+U8 = mybir.dt.uint8
+FP8X4 = mybir.dt.float8_e4m3fn_x4
+ALU = mybir.AluOpType
+ACT = mybir.ActivationFunctionType
+
+T, D, E = 8192, 1024, 128
+EPS = 1e-05
+FLOPS = 2 * T * D * 3 * E
+
+P = 128
+NT = T // P
+GT = 4
+NG = NT // GT
+GTOK = GT * P
+KP = 512
+NC = D // KP
+HBUFS = 8
+
+TS_ENG = ("g", "g", "g", "v")
+VSPLIT = 384
+
+
+def tile_toyattnsublayer_pa_t_kernel(tc, h, ln_w, ln_b, w_q, w_k, w_v, out_0, out_1, out_2):
+    nc = tc.nc
+    h_v = h.rearrange("(p n) k -> p n k", n=NT)
+    outs_v = [o.rearrange("(p n) e -> p n e", n=NT) for o in (out_0, out_1, out_2)]
+
+    with ExitStack() as ctx:
+        const = ctx.enter_context(tc.tile_pool(name="const", bufs=1))
+        hpool = ctx.enter_context(tc.tile_pool(name="hpool", bufs=HBUFS))
+        small = ctx.enter_context(tc.tile_pool(name="small", bufs=4))
+        xpool = ctx.enter_context(tc.tile_pool(name="xpool", bufs=3))
+        plpool = ctx.enter_context(tc.tile_pool(name="plpool", bufs=3))
+        grpool = ctx.enter_context(tc.tile_pool(name="grpool", bufs=3))
+        cpool = ctx.enter_context(tc.tile_pool(name="cpool", bufs=4))
+        opool = ctx.enter_context(tc.tile_pool(name="opool", bufs=3))
+        psum = ctx.enter_context(tc.psum_pool(name="psum", bufs=1))
+
+        hts = {}
+
+        def load(g):
+            ht = hpool.tile([P, GT, D], BF16, name="ht")
+            hts[g] = ht
+            if g == 0:
+                for i in range(GT):
+                    nc.sync.dma_start(out=ht[:, i, :], in_=h_v[:, i, :])
+            else:
+                nc.sync.dma_start(out=ht[:], in_=h_v[:, GT * g : GT * (g + 1), :])
+
+        ident_f = const.tile([P, P], F32, name="ident_f")
+        make_identity(nc, ident_f[:])
+        ident_b = const.tile([P, P], BF16, name="ident_b")
+        make_identity(nc, ident_b[:])
+        lnrows = const.tile([P, P], BF16, name="lnrows")
+        nc.vector.memset(lnrows[:], 0.0)
+        wg = const.tile([P, NC, 512, 4], BF16, name="wg", align_bytes=64)
+        nc.vector.memset(wg[:, :, 3 * E : 512, :], 0.0)
+
+        load(0)
+        nc.sync.dma_start(out=lnrows[0:8, :], in_=ln_w.rearrange("(r c) -> r c", c=P))
+        nc.sync.dma_start(out=lnrows[8:16, :], in_=ln_b.rearrange("(r c) -> r c", c=P))
+        wraw = const.tile([P, 3, D], BF16, name="wraw")
+        for s, w in enumerate((w_q, w_k, w_v)):
+            nc.sync.dma_start(out=wraw[:, s, :], in_=w)
+        for g in range(1, HBUFS):
+            load(g)
+
+        ln_ps = psum.tile([P, P], BF16, name="ln_ps", tag="T0")
+        nc.tensor.transpose(ln_ps[:], lnrows[:], ident_b[:])
+        wb = const.tile([P, 16], F32, name="wb")
+        nc.vector.tensor_copy(out=wb[:], in_=ln_ps[:, 0:16])
+
+        for c in range(NC):
+            for s in range(3):
+                wt = psum.tile([P, 4, E], BF16, name="wt", tag="O%d" % ((3 * c + s) % 4))
+                for j in range(4):
+                    k0 = KP * c + P * j
+                    nc.tensor.transpose(wt[:, j, :], wraw[:, s, k0 : k0 + P], ident_b[:])
+                nc.vector.tensor_copy(
+                    out=wg[:, c, E * s : E * (s + 1), :], in_=wt[:].rearrange("p j e -> p e j")
+                )
+        wcodes = const.tile([P, NC, 512], U32, name="wcodes", align_bytes=64)
+        wscales = const.tile([P, NC, 512], U8, name="wscales", align_bytes=64)
+        nc.vector.quantize_mx(
+            out=wcodes[:].rearrange("p c n -> p (c n)").bitcast(FP8X4),
+            scales=wscales[:].rearrange("p c n -> p (c n)"),
+            in_=wg[:].rearrange("p c n j -> p (c n j)"),
+        )
+
+        for g in range(NG):
+            ht = hts[g]
+            st = small.tile([P, GT, 2, 6], F32, name="st")
+            mv = small.tile([P, GT, 2], F32, name="mv")
+            for i in range(GT):
+                for a in range(2):
+                    nc.vector.bn_stats(out=st[:, i, a, :], in_=ht[:, i, 512 * a : 512 * (a + 1)])
+                nc.vector.bn_aggr(out=mv[:, i, :], in_=st[:, i, :, :].rearrange("p a b -> p (a b)"))
+            veps = small.tile([P, GT], F32, name="veps")
+            nc.gpsimd.tensor_scalar(
+                out=veps[:], in0=mv[:, :, 1], scalar1=1.0, scalar2=EPS, op0=ALU.mult, op1=ALU.add
+            )
+            negmu = small.tile([P, GT], F32, name="negmu")
+            nc.gpsimd.tensor_scalar(
+                out=negmu[:], in0=mv[:, :, 0], scalar1=-1.0, scalar2=0.0, op0=ALU.mult, op1=ALU.add
+            )
+            std = small.tile([P, GT], F32, name="std")
+            nc.scalar.activation(out=std[:], in_=veps[:], func=ACT.Sqrt)
+            rstd = small.tile([P, GT], F32, name="rstd")
+            nc.vector.reciprocal(rstd[:], std[:])
+
+            xh = xpool.tile([P, GT, D], F32, name="xh")
+            for i in range(GT):
+                eng = nc.gpsimd if TS_ENG[i] == "g" else nc.vector
+                eng.tensor_scalar(
+                    out=xh[:, i, :],
+                    in0=ht[:, i, :],
+                    scalar1=negmu[:, i : i + 1],
+                    scalar2=rstd[:, i : i + 1],
+                    op0=ALU.add,
+                    op1=ALU.mult,
+                )
+            if g + HBUFS < NG:
+                load(g + HBUFS)
+
+            acc = []
+            for c in range(NC):
+                pl = plpool.tile([P, 4, GTOK], BF16, name="pl")
+                for j in range(4):
+                    kb = 4 * c + j
+                    tp = psum.tile([P, GTOK], F32, name="tp", tag="T%d" % j)
+                    for i in range(GT):
+                        nc.tensor.transpose(
+                            tp[:, P * i : P * (i + 1)], xh[:, i, P * kb : P * (kb + 1)], ident_f[:]
+                        )
+                    nc.scalar.activation(
+                        out=pl[:, j, :],
+                        in_=tp[:],
+                        func=ACT.Identity,
+                        scale=wb[:, kb : kb + 1],
+                        bias=wb[:, 8 + kb : 9 + kb],
+                    )
+                gr = grpool.tile([P, GTOK, 4], BF16, name="gr", align_bytes=64)
+                nc.vector.tensor_copy(
+                    out=gr[:, 0:VSPLIT, :].rearrange("p (c i) t -> p c t i", i=4),
+                    in_=pl[:, :, 0:VSPLIT].rearrange("p t (c i) -> p c t i", i=4),
+                )
+                nc.scalar.copy(
+                    out=gr[:, VSPLIT:GTOK, :].rearrange("p (c i) t -> p c t i", i=4),
+                    in_=pl[:, :, VSPLIT:GTOK].rearrange("p t (c i) -> p c t i", i=4),
+                )
+                codes = cpool.tile([P, GTOK], U32, name="codes", align_bytes=64)
+                scl = cpool.tile([P, GTOK], U8, name="scl", align_bytes=64)
+                nc.vector.quantize_mx(
+                    out=codes[:].bitcast(FP8X4), scales=scl[:], in_=gr[:].rearrange("p n j -> p (n j)")
+                )
+                for i in range(GT):
+                    if c == 0:
+                        acc.append(psum.tile([P, 512], F32, name="acc%d" % i, tag="O%d" % i))
+                    nc.tensor.matmul_mx(
+                        out=acc[i][:],
+                        lhsT=codes[:, P * i : P * (i + 1)].bitcast(FP8X4),
+                        lhsT_scale=scl[:, P * i : P * (i + 1)],
+                        rhs=wcodes[:, c, :].bitcast(FP8X4),
+                        rhs_scale=wscales[:, c, :],
+                        start=(c == 0),
+                        stop=(c == NC - 1),
+                    )
+            ost = opool.tile([P, 3, GT, E], F32, name="ost")
+            for i in range(GT):
+                nc.scalar.copy(out=ost[:, :, i, :], in_=acc[i][:, 0 : 3 * E].rearrange("p (s e) -> p s e", s=3))
+            for s in range(3):
+                nc.sync.dma_start(out=outs_v[s][:, GT * g : GT * (g + 1), :], in_=ost[:, s, :, :])

@@ -164,6 +164,15 @@ def tile_toyattnsublayer_pa_t_kernel(tc, h, ln_w, ln_b, w_q, w_k, w_v, out_0, ou
                 for i in range(GT):
                     if c == 0:
                         acc.append(psum.tile([P, 512], F32, name="acc%d" % i, tag="O%d" % i))
+                        nc.tensor.matmul_mx(
+                            out=acc[i][:],
+                            lhsT=codes[:, P * i : P * (i + 1)].bitcast(FP8X4),
+                            lhsT_scale=scl[:, P * i : P * (i + 1)],
+                            rhs=wcodes[:, c, :].bitcast(FP8X4),
+                            rhs_scale=wscales[:, c, :],
+                            start=True,
+                            stop=True,
+                        )
                     nc.tensor.matmul_mx(
                         out=acc[i][:],
                         lhsT=codes[:, P * i : P * (i + 1)].bitcast(FP8X4),

@@ -24,8 +24,8 @@ KP = 512
 NC = D // KP
 HBUFS = 8
 
-TS_ENG = ("g", "g", "g", "v")
-VSPLIT = 384
+TS_ENG = ("v", "s", "v", "s")
+VSPLIT = 512
 
 
 def tile_toyattnsublayer_pa_t_kernel(tc, h, ln_w, ln_b, w_q, w_k, w_v, out_0, out_1, out_2):
@@ -104,29 +104,35 @@ def tile_toyattnsublayer_pa_t_kernel(tc, h, ln_w, ln_b, w_q, w_k, w_v, out_0, ou
                     nc.vector.bn_stats(out=st[:, i, a, :], in_=ht[:, i, 512 * a : 512 * (a + 1)])
                 nc.vector.bn_aggr(out=mv[:, i, :], in_=st[:, i, :, :].rearrange("p a b -> p (a b)"))
             veps = small.tile([P, GT], F32, name="veps")
-            nc.gpsimd.tensor_scalar(
-                out=veps[:], in0=mv[:, :, 1], scalar1=1.0, scalar2=EPS, op0=ALU.mult, op1=ALU.add
-            )
-            negmu = small.tile([P, GT], F32, name="negmu")
-            nc.gpsimd.tensor_scalar(
-                out=negmu[:], in0=mv[:, :, 0], scalar1=-1.0, scalar2=0.0, op0=ALU.mult, op1=ALU.add
-            )
+            nc.vector.tensor_scalar(out=veps[:], in0=mv[:, :, 1], scalar1=EPS, scalar2=None, op0=ALU.add)
             std = small.tile([P, GT], F32, name="std")
             nc.scalar.activation(out=std[:], in_=veps[:], func=ACT.Sqrt)
             rstd = small.tile([P, GT], F32, name="rstd")
             nc.vector.reciprocal(rstd[:], std[:])
+            nmr = small.tile([P, GT], F32, name="nmr")
+            nc.vector.scalar_tensor_tensor(
+                out=nmr[:], in0=mv[:, :, 0], scalar=-1.0, in1=rstd[:], op0=ALU.mult, op1=ALU.mult
+            )
 
             xh = xpool.tile([P, GT, D], F32, name="xh")
             for i in range(GT):
-                eng = nc.gpsimd if TS_ENG[i] == "g" else nc.vector
-                eng.tensor_scalar(
-                    out=xh[:, i, :],
-                    in0=ht[:, i, :],
-                    scalar1=negmu[:, i : i + 1],
-                    scalar2=rstd[:, i : i + 1],
-                    op0=ALU.add,
-                    op1=ALU.mult,
-                )
+                if TS_ENG[i] == "v":
+                    nc.vector.tensor_scalar(
+                        out=xh[:, i, :],
+                        in0=ht[:, i, :],
+                        scalar1=mv[:, i, 0:1],
+                        scalar2=rstd[:, i : i + 1],
+                        op0=ALU.subtract,
+                        op1=ALU.mult,
+                    )
+                else:
+                    nc.scalar.activation(
+                        out=xh[:, i, :],
+                        in_=ht[:, i, :],
+                        func=ACT.Identity,
+                        scale=rstd[:, i : i + 1],
+                        bias=nmr[:, i : i + 1],
+                    )
             if g + HBUFS < NG:
                 load(g + HBUFS)
 
@@ -152,10 +158,11 @@ def tile_toyattnsublayer_pa_t_kernel(tc, h, ln_w, ln_b, w_q, w_k, w_v, out_0, ou
                     out=gr[:, 0:VSPLIT, :].rearrange("p (c i) t -> p c t i", i=4),
                     in_=pl[:, :, 0:VSPLIT].rearrange("p t (c i) -> p c t i", i=4),
                 )
-                nc.scalar.copy(
-                    out=gr[:, VSPLIT:GTOK, :].rearrange("p (c i) t -> p c t i", i=4),
-                    in_=pl[:, :, VSPLIT:GTOK].rearrange("p t (c i) -> p c t i", i=4),
-                )
+                if VSPLIT < GTOK:
+                    nc.scalar.copy(
+                        out=gr[:, VSPLIT:GTOK, :].rearrange("p (c i) t -> p c t i", i=4),
+                        in_=pl[:, :, VSPLIT:GTOK].rearrange("p t (c i) -> p c t i", i=4),
+                    )
                 codes = cpool.tile([P, GTOK], U32, name="codes", align_bytes=64)
                 scl = cpool.tile([P, GTOK], U8, name="scl", align_bytes=64)
                 nc.vector.quantize_mx(
@@ -164,15 +171,6 @@ def tile_toyattnsublayer_pa_t_kernel(tc, h, ln_w, ln_b, w_q, w_k, w_v, out_0, ou
                 for i in range(GT):
                     if c == 0:
                         acc.append(psum.tile([P, 512], F32, name="acc%d" % i, tag="O%d" % i))
-                        nc.tensor.matmul_mx(
-                            out=acc[i][:],
-                            lhsT=codes[:, P * i : P * (i + 1)].bitcast(FP8X4),
-                            lhsT_scale=scl[:, P * i : P * (i + 1)],
-                            rhs=wcodes[:, c, :].bitcast(FP8X4),
-                            rhs_scale=wscales[:, c, :],
-                            start=True,
-                            stop=True,
-                        )
                     nc.tensor.matmul_mx(
                         out=acc[i][:],
                         lhsT=codes[:, P * i : P * (i + 1)].bitcast(FP8X4),

@@ -22,10 +22,28 @@ NG = NT // GT
 GTOK = GT * P
 KP = 512
 NC = D // KP
+NU = NG * NC
 HBUFS = 8
 
-TS_ENG = ("v", "s", "v", "s")
-VSPLIT = 512
+A0 = 5
+BV = 2
+BS = 1
+
+
+def n_scalar_norm(g):
+    if g == 0:
+        return 4
+    if g == NG - 1:
+        return 1
+    return 2
+
+
+def n_vector_leave(u):
+    return 1 if u >= 29 else 0
+
+
+def n_vector_out(g):
+    return 2 if g >= 12 else 0
 
 
 def tile_toyattnsublayer_pa_t_kernel(tc, h, ln_w, ln_b, w_q, w_k, w_v, out_0, out_1, out_2):
@@ -37,151 +55,252 @@ def tile_toyattnsublayer_pa_t_kernel(tc, h, ln_w, ln_b, w_q, w_k, w_v, out_0, ou
         const = ctx.enter_context(tc.tile_pool(name="const", bufs=1))
         hpool = ctx.enter_context(tc.tile_pool(name="hpool", bufs=HBUFS))
         small = ctx.enter_context(tc.tile_pool(name="small", bufs=4))
-        xpool = ctx.enter_context(tc.tile_pool(name="xpool", bufs=3))
+        xpool = ctx.enter_context(tc.tile_pool(name="xpool", bufs=2))
         plpool = ctx.enter_context(tc.tile_pool(name="plpool", bufs=3))
         grpool = ctx.enter_context(tc.tile_pool(name="grpool", bufs=3))
         cpool = ctx.enter_context(tc.tile_pool(name="cpool", bufs=4))
         opool = ctx.enter_context(tc.tile_pool(name="opool", bufs=3))
         psum = ctx.enter_context(tc.psum_pool(name="psum", bufs=1))
+        ctx.enter_context(tc.manual_schedule())
 
-        hts = {}
+        hts, sts, mvs, rstds, nmrs, xhs = {}, {}, {}, {}, {}, {}
+        tps, pls, grs, cds, scs, accs, osts = {}, {}, {}, {}, {}, {}, {}
 
-        def load(g):
-            ht = hpool.tile([P, GT, D], BF16, name="ht")
-            hts[g] = ht
-            if g == 0:
-                for i in range(GT):
-                    nc.sync.dma_start(out=ht[:, i, :], in_=h_v[:, i, :])
-            else:
+        def load(g, tiles=None):
+            if g not in hts:
+                hts[g] = hpool.tile([P, GT, D], BF16, name="ht")
+            ht = hts[g]
+            if tiles is None:
                 nc.sync.dma_start(out=ht[:], in_=h_v[:, GT * g : GT * (g + 1), :])
+            else:
+                for i in tiles:
+                    nc.sync.dma_start(out=ht[:, i, :], in_=h_v[:, GT * g + i, :])
 
-        ident_f = const.tile([P, P], F32, name="ident_f")
-        make_identity(nc, ident_f[:])
+        def stats(g, pairs):
+            if g not in sts:
+                sts[g] = small.tile([P, GT, 2, 6], F32, name="st")
+            for i, a in pairs:
+                nc.vector.bn_stats(out=sts[g][:, i, a, :], in_=hts[g][:, i, 512 * a : 512 * (a + 1)])
+
+        def aggregate(g):
+            mvs[g] = small.tile([P, GT, 2], F32, name="mv")
+            for i in range(GT):
+                nc.vector.bn_aggr(out=mvs[g][:, i, :], in_=sts[g][:, i, :, :].rearrange("p a b -> p (a b)"))
+
+        def chain(g):
+            mv = mvs[g]
+            veps = small.tile([P, GT], F32, name="veps")
+            nc.gpsimd.tensor_scalar(
+                out=veps[:], in0=mv[:, :, 1], scalar1=1.0, scalar2=EPS, op0=ALU.mult, op1=ALU.add
+            )
+            negmu = small.tile([P, GT], F32, name="negmu")
+            nc.gpsimd.tensor_scalar(
+                out=negmu[:], in0=mv[:, :, 0], scalar1=-1.0, scalar2=0.0, op0=ALU.mult, op1=ALU.add
+            )
+            rstds[g] = small.tile([P, GT], F32, name="rstd")
+            nc.gpsimd.tensor_tensor(out=rstds[g][:], in0=veps[:], in1=mhalf[:], op=ALU.pow)
+            nmrs[g] = small.tile([P, GT], F32, name="nmr")
+            nc.gpsimd.tensor_tensor(out=nmrs[g][:], in0=negmu[:], in1=rstds[g][:], op=ALU.mult)
+
+        def normalise(g, i, on_vector):
+            if g not in xhs:
+                xhs[g] = xpool.tile([P, GT, D], F32, name="xh")
+            if on_vector:
+                nc.vector.tensor_scalar(
+                    out=xhs[g][:, i, :],
+                    in0=hts[g][:, i, :],
+                    scalar1=mvs[g][:, i, 0:1],
+                    scalar2=rstds[g][:, i : i + 1],
+                    op0=ALU.subtract,
+                    op1=ALU.mult,
+                )
+            else:
+                nc.scalar.activation(
+                    out=xhs[g][:, i, :],
+                    in_=hts[g][:, i, :],
+                    func=ACT.Identity,
+                    scale=rstds[g][:, i : i + 1],
+                    bias=nmrs[g][:, i : i + 1],
+                )
+
+        def transposes(u, j):
+            g, c = divmod(u, NC)
+            kb = 4 * c + j
+            tp = psum.tile([P, GTOK], F32, name="tp", tag="T%d" % j)
+            tps[(u, j)] = tp
+            for i in range(GT):
+                nc.tensor.transpose(tp[:, P * i : P * (i + 1)], xhs[g][:, i, P * kb : P * (kb + 1)], ident_f[:])
+
+        def leave(u, j, on_vector):
+            kb = 4 * (u % NC) + j
+            if u not in pls:
+                pls[u] = plpool.tile([P, 4, GTOK], BF16, name="pl")
+            if on_vector:
+                nc.vector.tensor_scalar(
+                    out=pls[u][:, j, :],
+                    in0=tps[(u, j)][:],
+                    scalar1=wb[:, kb : kb + 1],
+                    scalar2=wb[:, 8 + kb : 9 + kb],
+                    op0=ALU.mult,
+                    op1=ALU.add,
+                )
+            else:
+                nc.scalar.activation(
+                    out=pls[u][:, j, :],
+                    in_=tps[(u, j)][:],
+                    func=ACT.Identity,
+                    scale=wb[:, kb : kb + 1],
+                    bias=wb[:, 8 + kb : 9 + kb],
+                )
+
+        def regroup(u):
+            grs[u] = grpool.tile([P, GTOK, 4], BF16, name="gr", align_bytes=64)
+            nc.vector.tensor_copy(
+                out=grs[u][:].rearrange("p (c i) t -> p c t i", i=4),
+                in_=pls[u][:].rearrange("p t (c i) -> p c t i", i=4),
+            )
+
+        def quantise(u):
+            cds[u] = cpool.tile([P, GTOK], U32, name="codes", align_bytes=64)
+            scs[u] = cpool.tile([P, GTOK], U8, name="scl", align_bytes=64)
+            nc.vector.quantize_mx(
+                out=cds[u][:].bitcast(FP8X4), scales=scs[u][:], in_=grs[u][:].rearrange("p n j -> p (n j)")
+            )
+
+        def multiply(u):
+            g, c = divmod(u, NC)
+            if c == 0:
+                accs[g] = [psum.tile([P, 512], F32, name="acc%d" % i, tag="O%d" % i) for i in range(GT)]
+            for i in range(GT):
+                nc.tensor.matmul_mx(
+                    out=accs[g][i][:],
+                    lhsT=cds[u][:, P * i : P * (i + 1)].bitcast(FP8X4),
+                    lhsT_scale=scs[u][:, P * i : P * (i + 1)],
+                    rhs=wcodes[:, c, :].bitcast(FP8X4),
+                    rhs_scale=wscales[:, c, :],
+                    start=(c == 0),
+                    stop=(c == NC - 1),
+                )
+
+        def out_copy(g, i, on_vector):
+            if g not in osts:
+                osts[g] = opool.tile([P, 3, GT, E], F32, name="ost")
+            src = accs[g][i][:, 0 : 3 * E].rearrange("p (s e) -> p s e", s=3)
+            if on_vector:
+                nc.vector.tensor_copy(out=osts[g][:, :, i, :], in_=src)
+            else:
+                nc.scalar.copy(out=osts[g][:, :, i, :], in_=src)
+
+        def store(g):
+            for s in range(3):
+                nc.sync.dma_start(out=outs_v[s][:, GT * g : GT * (g + 1), :], in_=osts[g][:, s, :, :])
+
         ident_b = const.tile([P, P], BF16, name="ident_b")
         make_identity(nc, ident_b[:])
+        ident_f = const.tile([P, P], F32, name="ident_f")
+        make_identity(nc, ident_f[:])
         lnrows = const.tile([P, P], BF16, name="lnrows")
         nc.vector.memset(lnrows[:], 0.0)
+        mhalf = const.tile([P, GT], F32, name="mhalf")
+        nc.vector.memset(mhalf[:], -0.5)
         wg = const.tile([P, NC, 512, 4], BF16, name="wg", align_bytes=64)
         nc.vector.memset(wg[:, :, 3 * E : 512, :], 0.0)
 
-        load(0)
+        load(0, (0, 1))
         nc.sync.dma_start(out=lnrows[0:8, :], in_=ln_w.rearrange("(r c) -> r c", c=P))
         nc.sync.dma_start(out=lnrows[8:16, :], in_=ln_b.rearrange("(r c) -> r c", c=P))
+        load(0, (2, 3))
         wraw = const.tile([P, 3, D], BF16, name="wraw")
         for s, w in enumerate((w_q, w_k, w_v)):
             nc.sync.dma_start(out=wraw[:, s, :], in_=w)
         for g in range(1, HBUFS):
             load(g)
 
-        ln_ps = psum.tile([P, P], BF16, name="ln_ps", tag="T0")
+        ln_ps = psum.tile([P, P], BF16, name="ln_ps", tag="O2")
         nc.tensor.transpose(ln_ps[:], lnrows[:], ident_b[:])
         wb = const.tile([P, 16], F32, name="wb")
-        nc.vector.tensor_copy(out=wb[:], in_=ln_ps[:, 0:16])
-
+        nc.scalar.copy(out=wb[:], in_=ln_ps[:, 0:16])
+        wtags = ("T0", "T1", "T2", "T3", "O0", "O1")
         for c in range(NC):
             for s in range(3):
-                wt = psum.tile([P, 4, E], BF16, name="wt", tag="O%d" % ((3 * c + s) % 4))
+                wt = psum.tile([P, 4, E], BF16, name="wt", tag=wtags[3 * c + s])
                 for j in range(4):
                     k0 = KP * c + P * j
                     nc.tensor.transpose(wt[:, j, :], wraw[:, s, k0 : k0 + P], ident_b[:])
-                nc.vector.tensor_copy(
-                    out=wg[:, c, E * s : E * (s + 1), :], in_=wt[:].rearrange("p j e -> p e j")
-                )
+                nc.scalar.copy(out=wg[:, c, E * s : E * (s + 1), :], in_=wt[:].rearrange("p j e -> p e j"))
         wcodes = const.tile([P, NC, 512], U32, name="wcodes", align_bytes=64)
         wscales = const.tile([P, NC, 512], U8, name="wscales", align_bytes=64)
-        nc.vector.quantize_mx(
-            out=wcodes[:].rearrange("p c n -> p (c n)").bitcast(FP8X4),
-            scales=wscales[:].rearrange("p c n -> p (c n)"),
-            in_=wg[:].rearrange("p c n j -> p (c n j)"),
-        )
 
-        for g in range(NG):
-            ht = hts[g]
-            st = small.tile([P, GT, 2, 6], F32, name="st")
-            mv = small.tile([P, GT, 2], F32, name="mv")
-            for i in range(GT):
-                for a in range(2):
-                    nc.vector.bn_stats(out=st[:, i, a, :], in_=ht[:, i, 512 * a : 512 * (a + 1)])
-                nc.vector.bn_aggr(out=mv[:, i, :], in_=st[:, i, :, :].rearrange("p a b -> p (a b)"))
-            veps = small.tile([P, GT], F32, name="veps")
-            nc.vector.tensor_scalar(out=veps[:], in0=mv[:, :, 1], scalar1=EPS, scalar2=None, op0=ALU.add)
-            std = small.tile([P, GT], F32, name="std")
-            nc.scalar.activation(out=std[:], in_=veps[:], func=ACT.Sqrt)
-            rstd = small.tile([P, GT], F32, name="rstd")
-            nc.vector.reciprocal(rstd[:], std[:])
-            nmr = small.tile([P, GT], F32, name="nmr")
-            nc.vector.scalar_tensor_tensor(
-                out=nmr[:], in0=mv[:, :, 0], scalar=-1.0, in1=rstd[:], op0=ALU.mult, op1=ALU.mult
-            )
+        for t in range(-A0, NU + 2):
+            in_u = 0 <= t < NU
+            prev_u = 0 <= t - 1 < NU
+            g_bs, r_bs = divmod(t + BS, 2)
+            g_bv, r_bv = divmod(t + BV, 2)
+            g_f, r_f = divmod(t - 3, 2)
+            do_bs = r_bs == 0 and 0 <= g_bs < NG
+            do_bv = r_bv == 0 and 0 <= g_bv < NG
+            do_f = r_f == 0 and 0 <= g_f < NG
+            n_vl = n_vector_leave(t) if in_u else 0
+            n_fs = GT - n_vector_out(g_f) if do_f else 0
 
-            xh = xpool.tile([P, GT, D], F32, name="xh")
-            for i in range(GT):
-                if TS_ENG[i] == "v":
-                    nc.vector.tensor_scalar(
-                        out=xh[:, i, :],
-                        in0=ht[:, i, :],
-                        scalar1=mv[:, i, 0:1],
-                        scalar2=rstd[:, i : i + 1],
-                        op0=ALU.subtract,
-                        op1=ALU.mult,
-                    )
-                else:
-                    nc.scalar.activation(
-                        out=xh[:, i, :],
-                        in_=ht[:, i, :],
-                        func=ACT.Identity,
-                        scale=rstd[:, i : i + 1],
-                        bias=nmr[:, i : i + 1],
-                    )
-            if g + HBUFS < NG:
-                load(g + HBUFS)
+            if do_bs:
+                for i in range(n_scalar_norm(g_bs)):
+                    normalise(g_bs, GT - 1 - i, False)
+                if g_bs + HBUFS < NG:
+                    load(g_bs + HBUFS)
+            for i in range(min(2, n_fs)):
+                out_copy(g_f, i, False)
+            late = []
+            for j in range(2):
+                if in_u and j >= 4 - n_vl:
+                    late.append(j)
+                elif in_u:
+                    leave(t, j, False)
+                    if t + 1 < NU:
+                        transposes(t + 1, j)
+                elif t == -1:
+                    transposes(0, j)
 
-            acc = []
-            for c in range(NC):
-                pl = plpool.tile([P, 4, GTOK], BF16, name="pl")
-                for j in range(4):
-                    kb = 4 * c + j
-                    tp = psum.tile([P, GTOK], F32, name="tp", tag="T%d" % j)
-                    for i in range(GT):
-                        nc.tensor.transpose(
-                            tp[:, P * i : P * (i + 1)], xh[:, i, P * kb : P * (kb + 1)], ident_f[:]
-                        )
-                    nc.scalar.activation(
-                        out=pl[:, j, :],
-                        in_=tp[:],
-                        func=ACT.Identity,
-                        scale=wb[:, kb : kb + 1],
-                        bias=wb[:, 8 + kb : 9 + kb],
-                    )
-                gr = grpool.tile([P, GTOK, 4], BF16, name="gr", align_bytes=64)
-                nc.vector.tensor_copy(
-                    out=gr[:, 0:VSPLIT, :].rearrange("p (c i) t -> p c t i", i=4),
-                    in_=pl[:, :, 0:VSPLIT].rearrange("p t (c i) -> p c t i", i=4),
-                )
-                if VSPLIT < GTOK:
-                    nc.scalar.copy(
-                        out=gr[:, VSPLIT:GTOK, :].rearrange("p (c i) t -> p c t i", i=4),
-                        in_=pl[:, :, VSPLIT:GTOK].rearrange("p t (c i) -> p c t i", i=4),
-                    )
-                codes = cpool.tile([P, GTOK], U32, name="codes", align_bytes=64)
-                scl = cpool.tile([P, GTOK], U8, name="scl", align_bytes=64)
+            g_s, second = divmod(t + A0, 2)
+            have_s = 0 <= g_s < NG
+            pairs = [(2 * second + i, a) for i in range(2) for a in range(2)]
+            if prev_u:
+                regroup(t - 1)
+            if have_s:
+                stats(g_s, pairs[0:2])
+            if t == -2:
                 nc.vector.quantize_mx(
-                    out=codes[:].bitcast(FP8X4), scales=scl[:], in_=gr[:].rearrange("p n j -> p (n j)")
+                    out=wcodes[:].rearrange("p c n -> p (c n)").bitcast(FP8X4),
+                    scales=wscales[:].rearrange("p c n -> p (c n)"),
+                    in_=wg[:].rearrange("p c n j -> p (c n j)"),
                 )
-                for i in range(GT):
-                    if c == 0:
-                        acc.append(psum.tile([P, 512], F32, name="acc%d" % i, tag="O%d" % i))
-                    nc.tensor.matmul_mx(
-                        out=acc[i][:],
-                        lhsT=codes[:, P * i : P * (i + 1)].bitcast(FP8X4),
-                        lhsT_scale=scl[:, P * i : P * (i + 1)],
-                        rhs=wcodes[:, c, :].bitcast(FP8X4),
-                        rhs_scale=wscales[:, c, :],
-                        start=(c == 0),
-                        stop=(c == NC - 1),
-                    )
-            ost = opool.tile([P, 3, GT, E], F32, name="ost")
-            for i in range(GT):
-                nc.scalar.copy(out=ost[:, :, i, :], in_=acc[i][:, 0 : 3 * E].rearrange("p (s e) -> p s e", s=3))
-            for s in range(3):
-                nc.sync.dma_start(out=outs_v[s][:, GT * g : GT * (g + 1), :], in_=ost[:, s, :, :])
+            if prev_u:
+                quantise(t - 1)
+                multiply(t - 1)
+            for i in range(2, n_fs):
+                out_copy(g_f, i, False)
+            for j in range(2, 4):
+                if in_u and j >= 4 - n_vl:
+                    late.append(j)
+                elif in_u:
+                    leave(t, j, False)
+                    if t + 1 < NU:
+                        transposes(t + 1, j)
+                elif t == -1:
+                    transposes(0, j)
+            for j in late:
+                leave(t, j, True)
+                if t + 1 < NU:
+                    transposes(t + 1, j)
+            if have_s:
+                stats(g_s, pairs[2:4])
+            if do_bv:
+                for i in range(GT - n_scalar_norm(g_bv)):
+                    normalise(g_bv, i, True)
+            if do_f:
+                for i in range(n_fs, GT):
+                    out_copy(g_f, i, True)
+                store(g_f)
+            if have_s and second == 1:
+                aggregate(g_s)
+                chain(g_s)

@@ -25,25 +25,30 @@ NC = D // KP
 NU = NG * NC
 HBUFS = 8
 
-A0 = 5
-BV = 2
+A0 = 7
+VE = 5
+SQ = 4
+RC = 3
+BV = 3
 BS = 1
+ML = 2
 
 
 def n_scalar_norm(g):
-    if g == 0:
+    if g < 2:
         return 4
-    if g == NG - 1:
-        return 1
-    return 2
-
-
-def n_vector_leave(u):
-    return 1 if u >= 29 else 0
+    if g >= 14:
+        return 0
+    return 3 if g % 3 == 0 else 2
 
 
 def n_vector_out(g):
     return 2 if g >= 12 else 0
+
+
+def group_of(t, lead):
+    g, r = divmod(t + lead, 2)
+    return g if r == 0 and 0 <= g < NG else None
 
 
 def tile_toyattnsublayer_pa_t_kernel(tc, h, ln_w, ln_b, w_q, w_k, w_v, out_0, out_1, out_2):
@@ -64,6 +69,7 @@ def tile_toyattnsublayer_pa_t_kernel(tc, h, ln_w, ln_b, w_q, w_k, w_v, out_0, ou
         ctx.enter_context(tc.manual_schedule())
 
         hts, sts, mvs, rstds, nmrs, xhs = {}, {}, {}, {}, {}, {}
+        vepss, stds = {}, {}
         tps, pls, grs, cds, scs, accs, osts = {}, {}, {}, {}, {}, {}, {}
 
         def load(g, tiles=None):
@@ -87,20 +93,23 @@ def tile_toyattnsublayer_pa_t_kernel(tc, h, ln_w, ln_b, w_q, w_k, w_v, out_0, ou
             for i in range(GT):
                 nc.vector.bn_aggr(out=mvs[g][:, i, :], in_=sts[g][:, i, :, :].rearrange("p a b -> p (a b)"))
 
-        def chain(g):
-            mv = mvs[g]
-            veps = small.tile([P, GT], F32, name="veps")
-            nc.gpsimd.tensor_scalar(
-                out=veps[:], in0=mv[:, :, 1], scalar1=1.0, scalar2=EPS, op0=ALU.mult, op1=ALU.add
-            )
-            negmu = small.tile([P, GT], F32, name="negmu")
-            nc.gpsimd.tensor_scalar(
-                out=negmu[:], in0=mv[:, :, 0], scalar1=-1.0, scalar2=0.0, op0=ALU.mult, op1=ALU.add
-            )
+        def add_eps(g):
+            vepss[g] = small.tile([P, GT], F32, name="veps")
+            nc.vector.tensor_scalar(out=vepss[g][:], in0=mvs[g][:, :, 1], scalar1=EPS, scalar2=None, op0=ALU.add)
+
+        def root(g):
+            stds[g] = small.tile([P, GT], F32, name="std")
+            nc.scalar.activation(out=stds[g][:], in_=vepss[g][:], func=ACT.Sqrt)
+
+        def reciprocal(g):
             rstds[g] = small.tile([P, GT], F32, name="rstd")
-            nc.gpsimd.tensor_tensor(out=rstds[g][:], in0=veps[:], in1=mhalf[:], op=ALU.pow)
+            nc.vector.reciprocal(rstds[g][:], stds[g][:])
+
+        def neg_mean_rstd(g):
             nmrs[g] = small.tile([P, GT], F32, name="nmr")
-            nc.gpsimd.tensor_tensor(out=nmrs[g][:], in0=negmu[:], in1=rstds[g][:], op=ALU.mult)
+            nc.vector.scalar_tensor_tensor(
+                out=nmrs[g][:], in0=mvs[g][:, :, 0], scalar=-1.0, in1=rstds[g][:], op0=ALU.mult, op1=ALU.mult
+            )
 
         def normalise(g, i, on_vector):
             if g not in xhs:
@@ -201,8 +210,6 @@ def tile_toyattnsublayer_pa_t_kernel(tc, h, ln_w, ln_b, w_q, w_k, w_v, out_0, ou
         make_identity(nc, ident_f[:])
         lnrows = const.tile([P, P], BF16, name="lnrows")
         nc.vector.memset(lnrows[:], 0.0)
-        mhalf = const.tile([P, GT], F32, name="mhalf")
-        nc.vector.memset(mhalf[:], -0.5)
         wg = const.tile([P, NC, 512, 4], BF16, name="wg", align_bytes=64)
         nc.vector.memset(wg[:, :, 3 * E : 512, :], 0.0)
 
@@ -231,41 +238,46 @@ def tile_toyattnsublayer_pa_t_kernel(tc, h, ln_w, ln_b, w_q, w_k, w_v, out_0, ou
         wcodes = const.tile([P, NC, 512], U32, name="wcodes", align_bytes=64)
         wscales = const.tile([P, NC, 512], U8, name="wscales", align_bytes=64)
 
-        for t in range(-A0, NU + 2):
+        for t in range(-A0, NU + ML + 1):
             in_u = 0 <= t < NU
             prev_u = 0 <= t - 1 < NU
-            g_bs, r_bs = divmod(t + BS, 2)
-            g_bv, r_bv = divmod(t + BV, 2)
-            g_f, r_f = divmod(t - 3, 2)
-            do_bs = r_bs == 0 and 0 <= g_bs < NG
-            do_bv = r_bv == 0 and 0 <= g_bv < NG
-            do_f = r_f == 0 and 0 <= g_f < NG
-            n_vl = n_vector_leave(t) if in_u else 0
-            n_fs = GT - n_vector_out(g_f) if do_f else 0
+            g_bs = group_of(t, BS)
+            g_bv = group_of(t, BV)
+            g_f = group_of(t, -(ML + 2))
+            g_ve = group_of(t, VE)
+            g_sq = group_of(t, SQ)
+            g_rc = group_of(t, RC)
+            g_s, second = divmod(t + A0, 2)
+            have_s = 0 <= g_s < NG
+            pairs = [(2 * second + i, a) for i in range(2) for a in range(2)]
+            n_fs = GT - n_vector_out(g_f) if g_f is not None else 0
 
-            if do_bs:
+            if g_sq is not None:
+                root(g_sq)
+            if g_bs is not None:
                 for i in range(n_scalar_norm(g_bs)):
                     normalise(g_bs, GT - 1 - i, False)
                 if g_bs + HBUFS < NG:
                     load(g_bs + HBUFS)
-            for i in range(min(2, n_fs)):
+            for i in range(n_fs):
                 out_copy(g_f, i, False)
-            late = []
-            for j in range(2):
-                if in_u and j >= 4 - n_vl:
-                    late.append(j)
-                elif in_u:
-                    leave(t, j, False)
-                    if t + 1 < NU:
-                        transposes(t + 1, j)
-                elif t == -1:
-                    transposes(0, j)
-
-            g_s, second = divmod(t + A0, 2)
-            have_s = 0 <= g_s < NG
-            pairs = [(2 * second + i, a) for i in range(2) for a in range(2)]
             if prev_u:
                 regroup(t - 1)
+            if g_f is not None:
+                for i in range(n_fs, GT):
+                    out_copy(g_f, i, True)
+                store(g_f)
+            for j in range(2):
+                if in_u:
+                    leave(t, j, False)
+                if -1 <= t < NU - 1:
+                    transposes(t + 1, j)
+            if 0 <= t - ML < NU:
+                multiply(t - ML)
+            if g_ve is not None:
+                add_eps(g_ve)
+            if g_rc is not None:
+                reciprocal(g_rc)
             if have_s:
                 stats(g_s, pairs[0:2])
             if t == -2:
@@ -276,31 +288,17 @@ def tile_toyattnsublayer_pa_t_kernel(tc, h, ln_w, ln_b, w_q, w_k, w_v, out_0, ou
                 )
             if prev_u:
                 quantise(t - 1)
-                multiply(t - 1)
-            for i in range(2, n_fs):
-                out_copy(g_f, i, False)
+            if g_rc is not None:
+                neg_mean_rstd(g_rc)
             for j in range(2, 4):
-                if in_u and j >= 4 - n_vl:
-                    late.append(j)
-                elif in_u:
+                if in_u:
                     leave(t, j, False)
-                    if t + 1 < NU:
-                        transposes(t + 1, j)
-                elif t == -1:
-                    transposes(0, j)
-            for j in late:
-                leave(t, j, True)
-                if t + 1 < NU:
+                if -1 <= t < NU - 1:
                     transposes(t + 1, j)
             if have_s:
                 stats(g_s, pairs[2:4])
-            if do_bv:
+            if g_bv is not None:
                 for i in range(GT - n_scalar_norm(g_bv)):
                     normalise(g_bv, i, True)
-            if do_f:
-                for i in range(n_fs, GT):
-                    out_copy(g_f, i, True)
-                store(g_f)
             if have_s and second == 1:
                 aggregate(g_s)
-                chain(g_s)

@@ -35,15 +35,21 @@ ML = 2
 
 
 def n_scalar_norm(g):
-    if g < 2:
+    if g == 0:
         return 4
-    if g >= 14:
-        return 0
-    return 3 if g % 3 == 0 else 2
+    if g >= 12:
+        return min(2, NG - 1 - g)
+    return 3 if g % 2 == 1 else 2
 
 
 def n_vector_out(g):
-    return 2 if g >= 12 else 0
+    if g >= 13:
+        return 2
+    return 1 if g >= 11 else 0
+
+
+def n_vector_leave(u):
+    return 1 if u in (28, 30) else 0
 
 
 def group_of(t, lead):
@@ -217,10 +223,11 @@ def tile_toyattnsublayer_pa_t_kernel(tc, h, ln_w, ln_b, w_q, w_k, w_v, out_0, ou
         nc.sync.dma_start(out=lnrows[0:8, :], in_=ln_w.rearrange("(r c) -> r c", c=P))
         nc.sync.dma_start(out=lnrows[8:16, :], in_=ln_b.rearrange("(r c) -> r c", c=P))
         load(0, (2, 3))
+        load(1)
         wraw = const.tile([P, 3, D], BF16, name="wraw")
         for s, w in enumerate((w_q, w_k, w_v)):
             nc.sync.dma_start(out=wraw[:, s, :], in_=w)
-        for g in range(1, HBUFS):
+        for g in range(2, HBUFS):
             load(g)
 
         ln_ps = psum.tile([P, P], BF16, name="ln_ps", tag="O2")
@@ -259,19 +266,17 @@ def tile_toyattnsublayer_pa_t_kernel(tc, h, ln_w, ln_b, w_q, w_k, w_v, out_0, ou
                     normalise(g_bs, GT - 1 - i, False)
                 if g_bs + HBUFS < NG:
                     load(g_bs + HBUFS)
-            for i in range(n_fs):
-                out_copy(g_f, i, False)
             if prev_u:
                 regroup(t - 1)
-            if g_f is not None:
-                for i in range(n_fs, GT):
-                    out_copy(g_f, i, True)
-                store(g_f)
             for j in range(2):
                 if in_u:
                     leave(t, j, False)
                 if -1 <= t < NU - 1:
                     transposes(t + 1, j)
+            if g_f is not None:
+                for i in range(GT):
+                    out_copy(g_f, i, i >= n_fs)
+                store(g_f)
             if 0 <= t - ML < NU:
                 multiply(t - ML)
             if g_ve is not None:
@@ -292,7 +297,7 @@ def tile_toyattnsublayer_pa_t_kernel(tc, h, ln_w, ln_b, w_q, w_k, w_v, out_0, ou
                 neg_mean_rstd(g_rc)
             for j in range(2, 4):
                 if in_u:
-                    leave(t, j, False)
+                    leave(t, j, j >= 4 - n_vector_leave(t))
                 if -1 <= t < NU - 1:
                     transposes(t + 1, j)
             if have_s:

@@ -35,7 +35,7 @@ ML = 2
 
 
 def n_scalar_norm(g):
-    if g == 0:
+    if g < 3:
         return 4
     if g >= 12:
         return min(2, NG - 1 - g)
@@ -43,13 +43,13 @@ def n_scalar_norm(g):
 
 
 def n_vector_out(g):
-    if g >= 13:
-        return 2
-    return 1 if g >= 11 else 0
+    if g < 11:
+        return 0
+    return 2 if g in (13, 15) else 1
 
 
 def n_vector_leave(u):
-    return 1 if u in (28, 30) else 0
+    return 1 if u == NU - 1 else 0
 
 
 def group_of(t, lead):
@@ -86,7 +86,10 @@ def tile_toyattnsublayer_pa_t_kernel(tc, h, ln_w, ln_b, w_q, w_k, w_v, out_0, ou
                 nc.sync.dma_start(out=ht[:], in_=h_v[:, GT * g : GT * (g + 1), :])
             else:
                 for i in tiles:
-                    nc.sync.dma_start(out=ht[:, i, :], in_=h_v[:, GT * g + i, :])
+                    n = 2 if i == 0 else 1
+                    for a in range(n):
+                        cols = slice(D // n * a, D // n * (a + 1))
+                        nc.sync.dma_start(out=ht[:, i, cols], in_=h_v[:, GT * g + i, cols])
 
         def stats(g, pairs):
             if g not in sts:
@@ -168,19 +171,27 @@ def tile_toyattnsublayer_pa_t_kernel(tc, h, ln_w, ln_b, w_q, w_k, w_v, out_0, ou
                     bias=wb[:, 8 + kb : 9 + kb],
                 )
 
+        def pieces(u):
+            n = 2 if u == NU - 1 else 1
+            return [slice(GTOK // n * a, GTOK // n * (a + 1)) for a in range(n)]
+
         def regroup(u):
             grs[u] = grpool.tile([P, GTOK, 4], BF16, name="gr", align_bytes=64)
-            nc.vector.tensor_copy(
-                out=grs[u][:].rearrange("p (c i) t -> p c t i", i=4),
-                in_=pls[u][:].rearrange("p t (c i) -> p c t i", i=4),
-            )
+            for tok in pieces(u):
+                nc.vector.tensor_copy(
+                    out=grs[u][:, tok, :].rearrange("p (c i) t -> p c t i", i=4),
+                    in_=pls[u][:, :, tok].rearrange("p t (c i) -> p c t i", i=4),
+                )
 
         def quantise(u):
             cds[u] = cpool.tile([P, GTOK], U32, name="codes", align_bytes=64)
             scs[u] = cpool.tile([P, GTOK], U8, name="scl", align_bytes=64)
-            nc.vector.quantize_mx(
-                out=cds[u][:].bitcast(FP8X4), scales=scs[u][:], in_=grs[u][:].rearrange("p n j -> p (n j)")
-            )
+            for tok in pieces(u):
+                nc.vector.quantize_mx(
+                    out=cds[u][:, tok].bitcast(FP8X4),
+                    scales=scs[u][:, tok],
+                    in_=grs[u][:, tok, :].rearrange("p n j -> p (n j)"),
+                )
 
         def multiply(u):
             g, c = divmod(u, NC)
@@ -291,19 +302,28 @@ def tile_toyattnsublayer_pa_t_kernel(tc, h, ln_w, ln_b, w_q, w_k, w_v, out_0, ou
                     scales=wscales[:].rearrange("p c n -> p (c n)"),
                     in_=wg[:].rearrange("p c n j -> p (c n j)"),
                 )
+            n_vl = n_vector_leave(t) if in_u else 0
+            if not have_s:
+                if g_bv is not None:
+                    for i in range(GT - n_scalar_norm(g_bv)):
+                        normalise(g_bv, i, True)
+                for j in range(4 - n_vl, 4):
+                    leave(t, j, True)
+                    if t < NU - 1:
+                        transposes(t + 1, j)
             if prev_u:
                 quantise(t - 1)
             if g_rc is not None:
                 neg_mean_rstd(g_rc)
-            for j in range(2, 4):
+            for j in range(2, 4 - n_vl):
                 if in_u:
-                    leave(t, j, j >= 4 - n_vector_leave(t))
+                    leave(t, j, False)
                 if -1 <= t < NU - 1:
                     transposes(t + 1, j)
             if have_s:
                 stats(g_s, pairs[2:4])
-            if g_bv is not None:
-                for i in range(GT - n_scalar_norm(g_bv)):
-                    normalise(g_bv, i, True)
+                if g_bv is not None:
+                    for i in range(GT - n_scalar_norm(g_bv)):
+                        normalise(g_bv, i, True)
             if have_s and second == 1:
                 aggregate(g_s)

@@ -26,7 +26,6 @@ NU = NG * NC
 HBUFS = 8
 
 A0 = 7
-VE = 5
 SQ = 4
 RC = 3
 BV = 3
@@ -75,7 +74,7 @@ def tile_toyattnsublayer_pa_t_kernel(tc, h, ln_w, ln_b, w_q, w_k, w_v, out_0, ou
         ctx.enter_context(tc.manual_schedule())
 
         hts, sts, mvs, rstds, nmrs, xhs = {}, {}, {}, {}, {}, {}
-        vepss, stds = {}, {}
+        stds = {}
         tps, pls, grs, cds, scs, accs, osts = {}, {}, {}, {}, {}, {}, {}
 
         def load(g, tiles=None):
@@ -102,13 +101,9 @@ def tile_toyattnsublayer_pa_t_kernel(tc, h, ln_w, ln_b, w_q, w_k, w_v, out_0, ou
             for i in range(GT):
                 nc.vector.bn_aggr(out=mvs[g][:, i, :], in_=sts[g][:, i, :, :].rearrange("p a b -> p (a b)"))
 
-        def add_eps(g):
-            vepss[g] = small.tile([P, GT], F32, name="veps")
-            nc.vector.tensor_scalar(out=vepss[g][:], in0=mvs[g][:, :, 1], scalar1=EPS, scalar2=None, op0=ALU.add)
-
         def root(g):
             stds[g] = small.tile([P, GT], F32, name="std")
-            nc.scalar.activation(out=stds[g][:], in_=vepss[g][:], func=ACT.Sqrt)
+            nc.scalar.activation(out=stds[g][:], in_=mvs[g][:, :, 1], func=ACT.Sqrt, bias=eps_t[:, 0:1], scale=1.0)
 
         def reciprocal(g):
             rstds[g] = small.tile([P, GT], F32, name="rstd")
@@ -227,6 +222,9 @@ def tile_toyattnsublayer_pa_t_kernel(tc, h, ln_w, ln_b, w_q, w_k, w_v, out_0, ou
         make_identity(nc, ident_f[:])
         lnrows = const.tile([P, P], BF16, name="lnrows")
         nc.vector.memset(lnrows[:], 0.0)
+        eps_t = const.tile([P, 1], F32, name="eps_t")
+        nc.vector.memset(eps_t[:], 0.0)
+        nc.vector.tensor_scalar(out=eps_t[:], in0=eps_t[:], scalar1=EPS, scalar2=None, op0=ALU.add)
         wg = const.tile([P, NC, 512, 4], BF16, name="wg", align_bytes=64)
         nc.vector.memset(wg[:, :, 3 * E : 512, :], 0.0)
 
@@ -262,7 +260,6 @@ def tile_toyattnsublayer_pa_t_kernel(tc, h, ln_w, ln_b, w_q, w_k, w_v, out_0, ou
             g_bs = group_of(t, BS)
             g_bv = group_of(t, BV)
             g_f = group_of(t, -(ML + 2))
-            g_ve = group_of(t, VE)
             g_sq = group_of(t, SQ)
             g_rc = group_of(t, RC)
             g_s, second = divmod(t + A0, 2)
@@ -290,8 +287,6 @@ def tile_toyattnsublayer_pa_t_kernel(tc, h, ln_w, ln_b, w_q, w_k, w_v, out_0, ou
                 store(g_f)
             if 0 <= t - ML < NU:
                 multiply(t - ML)
-            if g_ve is not None:
-                add_eps(g_ve)
             if g_rc is not None:
                 reciprocal(g_rc)
             if have_s:
@@ -313,7 +308,7 @@ def tile_toyattnsublayer_pa_t_kernel(tc, h, ln_w, ln_b, w_q, w_k, w_v, out_0, ou
                         transposes(t + 1, j)
             if prev_u:
                 quantise(t - 1)
-            if g_rc is not None:
+            if g_rc is not None and n_scalar_norm(g_rc) > 0:
                 neg_mean_rstd(g_rc)
             for j in range(2, 4 - n_vl):
                 if in_u:

from contextlib import ExitStack

import concourse.mybir as mybir
from concourse.masks import make_identity

F32 = mybir.dt.float32
BF16 = mybir.dt.bfloat16
U32 = mybir.dt.uint32
U8 = mybir.dt.uint8
FP8X4 = mybir.dt.float8_e4m3fn_x4
ALU = mybir.AluOpType
ACT = mybir.ActivationFunctionType

T, D, E = 8192, 1024, 128
EPS = 1e-05
FLOPS = 2 * T * D * 3 * E

P = 128
NT = T // P
GT = 4
NG = NT // GT
GTOK = GT * P
KP = 512
NC = D // KP
NU = NG * NC
HBUFS = 8

A0 = 7
SQ = 4
RC = 3
BV = 3
BS = 1
ML = 2


def n_scalar_norm(g):
    if g < 3:
        return 4
    if g >= 12:
        return min(2, NG - 1 - g)
    return 3 if g % 2 == 1 else 2


def n_vector_out(g):
    if g < 11:
        return 0
    return 2 if g in (13, 15) else 1


def n_vector_leave(u):
    return 1 if u == NU - 1 else 0


def group_of(t, lead):
    g, r = divmod(t + lead, 2)
    return g if r == 0 and 0 <= g < NG else None


def tile_toyattnsublayer_pa_t_kernel(tc, h, ln_w, ln_b, w_q, w_k, w_v, out_0, out_1, out_2):
    nc = tc.nc
    h_v = h.rearrange("(p n) k -> p n k", n=NT)
    outs_v = [o.rearrange("(p n) e -> p n e", n=NT) for o in (out_0, out_1, out_2)]

    with ExitStack() as ctx:
        const = ctx.enter_context(tc.tile_pool(name="const", bufs=1))
        hpool = ctx.enter_context(tc.tile_pool(name="hpool", bufs=HBUFS))
        small = ctx.enter_context(tc.tile_pool(name="small", bufs=4))
        xpool = ctx.enter_context(tc.tile_pool(name="xpool", bufs=2))
        plpool = ctx.enter_context(tc.tile_pool(name="plpool", bufs=3))
        grpool = ctx.enter_context(tc.tile_pool(name="grpool", bufs=3))
        cpool = ctx.enter_context(tc.tile_pool(name="cpool", bufs=4))
        opool = ctx.enter_context(tc.tile_pool(name="opool", bufs=3))
        psum = ctx.enter_context(tc.psum_pool(name="psum", bufs=1))
        ctx.enter_context(tc.manual_schedule())

        hts, sts, mvs, rstds, nmrs, xhs = {}, {}, {}, {}, {}, {}
        stds = {}
        tps, pls, grs, cds, scs, accs, osts = {}, {}, {}, {}, {}, {}, {}

        def load(g, tiles=None):
            if g not in hts:
                hts[g] = hpool.tile([P, GT, D], BF16, name="ht")
            ht = hts[g]
            if tiles is None:
                nc.sync.dma_start(out=ht[:], in_=h_v[:, GT * g : GT * (g + 1), :])
            else:
                for i in tiles:
                    n = 2 if i == 0 else 1
                    for a in range(n):
                        cols = slice(D // n * a, D // n * (a + 1))
                        nc.sync.dma_start(out=ht[:, i, cols], in_=h_v[:, GT * g + i, cols])

        def stats(g, pairs):
            if g not in sts:
                sts[g] = small.tile([P, GT, 2, 6], F32, name="st")
            for i, a in pairs:
                nc.vector.bn_stats(out=sts[g][:, i, a, :], in_=hts[g][:, i, 512 * a : 512 * (a + 1)])

        def aggregate(g):
            mvs[g] = small.tile([P, GT, 2], F32, name="mv")
            for i in range(GT):
                nc.vector.bn_aggr(out=mvs[g][:, i, :], in_=sts[g][:, i, :, :].rearrange("p a b -> p (a b)"))

        def root(g):
            stds[g] = small.tile([P, GT], F32, name="std")
            nc.scalar.activation(out=stds[g][:], in_=mvs[g][:, :, 1], func=ACT.Sqrt, bias=eps_t[:, 0:1], scale=1.0)

        def reciprocal(g):
            rstds[g] = small.tile([P, GT], F32, name="rstd")
            nc.vector.reciprocal(rstds[g][:], stds[g][:])

        def neg_mean_rstd(g):
            nmrs[g] = small.tile([P, GT], F32, name="nmr")
            nc.vector.scalar_tensor_tensor(
                out=nmrs[g][:], in0=mvs[g][:, :, 0], scalar=-1.0, in1=rstds[g][:], op0=ALU.mult, op1=ALU.mult
            )

        def normalise(g, i, on_vector):
            if g not in xhs:
                xhs[g] = xpool.tile([P, GT, D], F32, name="xh")
            if on_vector:
                nc.vector.tensor_scalar(
                    out=xhs[g][:, i, :],
                    in0=hts[g][:, i, :],
                    scalar1=mvs[g][:, i, 0:1],
                    scalar2=rstds[g][:, i : i + 1],
                    op0=ALU.subtract,
                    op1=ALU.mult,
                )
            else:
                nc.scalar.activation(
                    out=xhs[g][:, i, :],
                    in_=hts[g][:, i, :],
                    func=ACT.Identity,
                    scale=rstds[g][:, i : i + 1],
                    bias=nmrs[g][:, i : i + 1],
                )

        def transposes(u, j):
            g, c = divmod(u, NC)
            kb = 4 * c + j
            tp = psum.tile([P, GTOK], F32, name="tp", tag="T%d" % j)
            tps[(u, j)] = tp
            for i in range(GT):
                nc.tensor.transpose(tp[:, P * i : P * (i + 1)], xhs[g][:, i, P * kb : P * (kb + 1)], ident_f[:])

        def leave(u, j, on_vector):
            kb = 4 * (u % NC) + j
            if u not in pls:
                pls[u] = plpool.tile([P, 4, GTOK], BF16, name="pl")
            if on_vector:
                nc.vector.tensor_scalar(
                    out=pls[u][:, j, :],
                    in0=tps[(u, j)][:],
                    scalar1=wb[:, kb : kb + 1],
                    scalar2=wb[:, 8 + kb : 9 + kb],
                    op0=ALU.mult,
                    op1=ALU.add,
                )
            else:
                nc.scalar.activation(
                    out=pls[u][:, j, :],
                    in_=tps[(u, j)][:],
                    func=ACT.Identity,
                    scale=wb[:, kb : kb + 1],
                    bias=wb[:, 8 + kb : 9 + kb],
                )

        def pieces(u):
            n = 2 if u == NU - 1 else 1
            return [slice(GTOK // n * a, GTOK // n * (a + 1)) for a in range(n)]

        def regroup(u):
            grs[u] = grpool.tile([P, GTOK, 4], BF16, name="gr", align_bytes=64)
            for tok in pieces(u):
                nc.vector.tensor_copy(
                    out=grs[u][:, tok, :].rearrange("p (c i) t -> p c t i", i=4),
                    in_=pls[u][:, :, tok].rearrange("p t (c i) -> p c t i", i=4),
                )

        def quantise(u):
            cds[u] = cpool.tile([P, GTOK], U32, name="codes", align_bytes=64)
            scs[u] = cpool.tile([P, GTOK], U8, name="scl", align_bytes=64)
            for tok in pieces(u):
                nc.vector.quantize_mx(
                    out=cds[u][:, tok].bitcast(FP8X4),
                    scales=scs[u][:, tok],
                    in_=grs[u][:, tok, :].rearrange("p n j -> p (n j)"),
                )

        def multiply(u):
            g, c = divmod(u, NC)
            if c == 0:
                accs[g] = [psum.tile([P, 512], F32, name="acc%d" % i, tag="O%d" % i) for i in range(GT)]
            for i in range(GT):
                nc.tensor.matmul_mx(
                    out=accs[g][i][:],
                    lhsT=cds[u][:, P * i : P * (i + 1)].bitcast(FP8X4),
                    lhsT_scale=scs[u][:, P * i : P * (i + 1)],
                    rhs=wcodes[:, c, :].bitcast(FP8X4),
                    rhs_scale=wscales[:, c, :],
                    start=(c == 0),
                    stop=(c == NC - 1),
                )

        def out_copy(g, i, on_vector):
            if g not in osts:
                osts[g] = opool.tile([P, 3, GT, E], F32, name="ost")
            src = accs[g][i][:, 0 : 3 * E].rearrange("p (s e) -> p s e", s=3)
            if on_vector:
                nc.vector.tensor_copy(out=osts[g][:, :, i, :], in_=src)
            else:
                nc.scalar.copy(out=osts[g][:, :, i, :], in_=src)

        def store(g):
            for s in range(3):
                nc.sync.dma_start(out=outs_v[s][:, GT * g : GT * (g + 1), :], in_=osts[g][:, s, :, :])

        ident_b = const.tile([P, P], BF16, name="ident_b")
        make_identity(nc, ident_b[:])
        ident_f = const.tile([P, P], F32, name="ident_f")
        make_identity(nc, ident_f[:])
        lnrows = const.tile([P, P], BF16, name="lnrows")
        nc.vector.memset(lnrows[:], 0.0)
        eps_t = const.tile([P, 1], F32, name="eps_t")
        nc.vector.memset(eps_t[:], 0.0)
        nc.vector.tensor_scalar(out=eps_t[:], in0=eps_t[:], scalar1=EPS, scalar2=None, op0=ALU.add)
        wg = const.tile([P, NC, 512, 4], BF16, name="wg", align_bytes=64)
        nc.vector.memset(wg[:, :, 3 * E : 512, :], 0.0)

        load(0, (0, 1))
        nc.sync.dma_start(out=lnrows[0:8, :], in_=ln_w.rearrange("(r c) -> r c", c=P))
        nc.sync.dma_start(out=lnrows[8:16, :], in_=ln_b.rearrange("(r c) -> r c", c=P))
        load(0, (2, 3))
        load(1)
        wraw = const.tile([P, 3, D], BF16, name="wraw")
        for s, w in enumerate((w_q, w_k, w_v)):
            nc.sync.dma_start(out=wraw[:, s, :], in_=w)
        for g in range(2, HBUFS):
            load(g)

        ln_ps = psum.tile([P, P], BF16, name="ln_ps", tag="O2")
        nc.tensor.transpose(ln_ps[:], lnrows[:], ident_b[:])
        wb = const.tile([P, 16], F32, name="wb")
        nc.scalar.copy(out=wb[:], in_=ln_ps[:, 0:16])
        wtags = ("T0", "T1", "T2", "T3", "O0", "O1")
        for c in range(NC):
            for s in range(3):
                wt = psum.tile([P, 4, E], BF16, name="wt", tag=wtags[3 * c + s])
                for j in range(4):
                    k0 = KP * c + P * j
                    nc.tensor.transpose(wt[:, j, :], wraw[:, s, k0 : k0 + P], ident_b[:])
                nc.scalar.copy(out=wg[:, c, E * s : E * (s + 1), :], in_=wt[:].rearrange("p j e -> p e j"))
        wcodes = const.tile([P, NC, 512], U32, name="wcodes", align_bytes=64)
        wscales = const.tile([P, NC, 512], U8, name="wscales", align_bytes=64)

        for t in range(-A0, NU + ML + 1):
            in_u = 0 <= t < NU
            prev_u = 0 <= t - 1 < NU
            g_bs = group_of(t, BS)
            g_bv = group_of(t, BV)
            g_f = group_of(t, -(ML + 2))
            g_sq = group_of(t, SQ)
            g_rc = group_of(t, RC)
            g_s, second = divmod(t + A0, 2)
            have_s = 0 <= g_s < NG
            pairs = [(2 * second + i, a) for i in range(2) for a in range(2)]
            n_fs = GT - n_vector_out(g_f) if g_f is not None else 0

            if g_sq is not None:
                root(g_sq)
            if g_bs is not None:
                for i in range(n_scalar_norm(g_bs)):
                    normalise(g_bs, GT - 1 - i, False)
                if g_bs + HBUFS < NG:
                    load(g_bs + HBUFS)
            if prev_u:
                regroup(t - 1)
            for j in range(2):
                if in_u:
                    leave(t, j, False)
                if -1 <= t < NU - 1:
                    transposes(t + 1, j)
            if g_f is not None:
                for i in range(GT):
                    out_copy(g_f, i, i >= n_fs)
                store(g_f)
            if 0 <= t - ML < NU:
                multiply(t - ML)
            if g_rc is not None:
                reciprocal(g_rc)
            if have_s:
                stats(g_s, pairs[0:2])
            if t == -2:
                nc.vector.quantize_mx(
                    out=wcodes[:].rearrange("p c n -> p (c n)").bitcast(FP8X4),
                    scales=wscales[:].rearrange("p c n -> p (c n)"),
                    in_=wg[:].rearrange("p c n j -> p (c n j)"),
                )
            n_vl = n_vector_leave(t) if in_u else 0
            if not have_s:
                if g_bv is not None:
                    for i in range(GT - n_scalar_norm(g_bv)):
                        normalise(g_bv, i, True)
                for j in range(4 - n_vl, 4):
                    leave(t, j, True)
                    if t < NU - 1:
                        transposes(t + 1, j)
            if prev_u:
                quantise(t - 1)
            if g_rc is not None and n_scalar_norm(g_rc) > 0:
                neg_mean_rstd(g_rc)
            for j in range(2, 4 - n_vl):
                if in_u:
                    leave(t, j, False)
                if -1 <= t < NU - 1:
                    transposes(t + 1, j)
            if have_s:
                stats(g_s, pairs[2:4])
                if g_bv is not None:
                    for i in range(GT - n_scalar_norm(g_bv)):
                        normalise(g_bv, i, True)
            if have_s and second == 1:
                aggregate(g_s)
